import numpy as np
import ml_dtypes


def mxq(x, axis, fmt="e4m3"):
    dtype, down = {"e4m3": (ml_dtypes.float8_e4m3fn, 7), "e5m2": (ml_dtypes.float8_e5m2, 14)}[fmt]
    v = np.moveaxis(np.asarray(x, np.float32).astype(ml_dtypes.bfloat16).astype(np.float64), axis, -1)
    blocks = v.reshape(v.shape[:-1] + (-1, 32))
    amax = np.abs(blocks).max(-1, keepdims=True)
    byte = np.maximum(np.where(amax > 0, np.frexp(amax)[1] - 1 + 127, 0) - down, 1)
    scale = np.exp2(byte - 127.0)
    codes = (blocks / scale).astype(np.float32).astype(dtype).astype(np.float64)
    return np.moveaxis((codes * scale).reshape(v.shape), -1, axis)


WIDE = False


def mx_kscale(k):
    if not WIDE:
        return np.ones(k)
    levels = np.array([10, -10, 5, -5, 0])
    a = np.random.permutation(np.resize(levels, k // 512 * 4)).reshape(k // 512, 4)
    idx = np.arange(k)
    return np.exp2(a[idx // 512, idx % 128 // 32])


BF16 = ml_dtypes.bfloat16


def bf(x):
    return np.asarray(x, np.float32).astype(BF16)


def f64(x):
    return np.asarray(x).astype(np.float64)


B, D, O, NC, NE, R = 16384, 512, 8, 8, 8, 8
C = NC + NE


def mix(z, u):
    return sum(z[..., r:r + 1] * u[r] for r in range(R))


def setup_inputs():
    u = np.random.standard_normal((R, D)) / np.sqrt(D)
    x = mix(np.random.standard_normal((B, R)) / np.sqrt(R), u) + 0.3 * np.random.standard_normal((B, D)) / np.sqrt(D)
    means = mix(np.random.standard_normal((O, C, R)) / np.sqrt(R), u) + 0.3 * np.random.standard_normal((O, C, D)) / np.sqrt(D)
    t = np.maximum(mx_kscale(D)[np.random.randint(0, D, (O, C))], 1.0) ** 2
    means = means * t[:, :, None]
    rho = np.random.uniform(-0.25, 0.75, (O, C))
    return {"x": bf(x), "means": bf(means), "rho": bf(rho)}


def reference(x, means, rho):
    x, means, rho = f64(x), f64(means), f64(rho)
    sigma = np.log1p(np.exp(rho))
    inv_2s2 = 1.0 / (2.0 * sigma * sigma)
    x2 = np.sum(x * x, axis=1)
    m2 = np.sum(means * means, axis=2)
    xm = (mxq(x, 1, "e4m3") @ mxq(means, 2, "e4m3").reshape(O * C, D).T).reshape(B, O, C)
    dist = x2[:, None, None] + m2[None, :, :] - 2.0 * xm
    Gall = np.exp(-dist * inv_2s2[None, :, :])
    G = Gall[:, :, :NC]
    N = Gall[:, :, NC:]
    P = (np.max(G, axis=2) * (NC + 1) - np.sum(G, axis=2)) / NC
    neg_P = np.sum(N, axis=2) / NE
    return P - neg_P

@@ -1,0 +1,368 @@
+from contextlib import ExitStack
+
+import concourse.mybir as mybir
+from concourse.masks import make_identity
+
+F32 = mybir.dt.float32
+BF16 = mybir.dt.bfloat16
+U32 = mybir.dt.uint32
+U8 = mybir.dt.uint8
+FP8X4 = mybir.dt.float8_e4m3fn_x4
+ACT = mybir.ActivationFunctionType
+ALU = mybir.AluOpType
+AX = mybir.AxisListType
+
+P = 128
+B = 16384
+D = 512
+O = 8
+C = 16
+NC = 8
+ROWS_PER_PART = 8
+CHUNK = P * ROWS_PER_PART
+QUAD = 4
+N_QUADS = B // (QUAD * P)
+GROUP = 4
+WORDS = D // 2
+SUM_COLS = 48
+SERIES = 11
+G_QUADS = (9, 17, 25)
+G_FIRST_STEP = 1
+S_COPIES = (6, 11, 16, 21, 26)
+S_LEAD = 14
+
+FLOPS = 2 * B * O * C * D
+
+
+def tile_vertical_space_layer_t_kernel(tc, x, means, rho, out):
+    nc = tc.nc
+    with ExitStack() as ctx:
+        const = ctx.enter_context(tc.tile_pool(name="const", bufs=1))
+        xpool = ctx.enter_context(tc.tile_pool(name="xpool", bufs=N_QUADS))
+        work = ctx.enter_context(tc.tile_pool(name="work", bufs=3))
+        psum = ctx.enter_context(tc.psum_pool(name="psum", bufs=1))
+        ctx.enter_context(tc.manual_schedule())
+
+        rho_sb = const.tile([P, 1], BF16)
+        with nc.allow_non_contiguous_dma(reason="128 single bf16 values, once"):
+            nc.scalar.dma_start(out=rho_sb[:], in_=rho.rearrange("o (c u) -> (o c) u", u=1))
+        m_sb = const.tile([P, D], BF16)
+        xq = {}
+        load_order = [0, 1, 2, G_QUADS[0]] + [q for q in range(3, N_QUADS) if q != G_QUADS[0]]
+        for q in load_order:
+            c, h = divmod(q, ROWS_PER_PART // QUAD)
+            xt = xpool.tile([P, QUAD * D], BF16, name="xt")
+            src = x[c * CHUNK : (c + 1) * CHUNK, :].rearrange("(p j) d -> p j d", j=ROWS_PER_PART)
+            dst = xt[:].rearrange("p (j d) -> p j d", d=D)
+            if q == 0:
+                for jj in range(QUAD):
+                    nc.sync.dma_start(out=dst[:, jj : jj + 1, :], in_=src[:, jj : jj + 1, :])
+                nc.sync.dma_start(out=m_sb[:], in_=means.rearrange("o c d -> (o c) d"))
+            else:
+                nc.sync.dma_start(out=dst, in_=src[:, h * QUAD : (h + 1) * QUAD, :])
+            xq[q] = xt
+
+        one = const.tile([P, 1], F32)
+        nc.vector.memset(one[:], 1.0)
+        warm = const.tile([P, 1], F32)
+        nc.scalar.activation(out=warm[:], in_=one[:], func=ACT.Exp)
+        ident = const.tile([P, P], F32)
+        make_identity(nc, ident[:])
+        class8 = const.tile([P, O], F32)
+        nc.vector.tensor_reduce(
+            out=class8[:], in_=ident[:].rearrange("p (o c) -> p o c", c=C), op=ALU.add, axis=AX.X
+        )
+        class_sum = const.tile([P, SUM_COLS], F32)
+        nc.vector.memset(class_sum[:], 0.0)
+        nc.vector.tensor_scalar_mul(out=class_sum[:, 0:O], in0=class8[:], scalar1=1.0 / NC)
+
+        rho_f = const.tile([P, 1], F32)
+        nc.vector.tensor_copy(out=rho_f[:], in_=rho_sb[:])
+        rho_n = const.tile([P, 1], F32)
+        nc.vector.tensor_scalar_mul(out=rho_n[:], in0=rho_f[:], scalar1=-1.0)
+        nabs = const.tile([P, 1], F32)
+        nc.vector.tensor_tensor(out=nabs[:], in0=rho_f[:], in1=rho_n[:], op=ALU.min)
+        relu = const.tile([P, 1], F32)
+        nc.vector.tensor_scalar_max(out=relu[:], in0=rho_f[:], scalar1=0.0)
+        t_small = const.tile([P, 1], F32)
+        nc.scalar.activation(out=t_small[:], in_=nabs[:], func=ACT.Exp)
+        den = const.tile([P, 1], F32)
+        nc.vector.tensor_scalar_add(out=den[:], in0=t_small[:], scalar1=2.0)
+        rden = const.tile([P, 1], F32)
+        nc.vector.reciprocal(out=rden[:], in_=den[:])
+        u_small = const.tile([P, 1], F32)
+        nc.vector.tensor_mul(out=u_small[:], in0=t_small[:], in1=rden[:])
+        u2 = const.tile([P, 1], F32)
+        nc.vector.tensor_mul(out=u2[:], in0=u_small[:], in1=u_small[:])
+        horner = [const.tile([P, 1], F32, name="horner%d" % i) for i in range(2)]
+        nc.gpsimd.tensor_scalar(
+            out=horner[0][:], in0=u2[:], scalar1=1.0 / (2 * SERIES - 1), scalar2=1.0 / (2 * SERIES - 3),
+            op0=ALU.mult, op1=ALU.add,
+        )
+        for i in range(SERIES - 2):
+            nc.gpsimd.tensor_scalar(
+                out=horner[(i + 1) % 2][:], in0=horner[i % 2][:], scalar1=u2[:], scalar2=1.0 / (2 * (SERIES - 3 - i) + 1),
+                op0=ALU.mult, op1=ALU.add,
+            )
+        series = horner[(SERIES - 2) % 2]
+        m2 = const.tile([P, 1], F32)
+        m_junk = const.tile([P, D], BF16)
+        sigma = const.tile([P, 1], F32)
+        s2 = const.tile([P, 1], F32)
+        neg_inv = const.tile([P, 1], F32)
+        exp_bias = const.tile([P, 1], F32)
+
+        def widths():
+            nc.vector.tensor_mul(out=sigma[:], in0=u_small[:], in1=series[:])
+            nc.vector.scalar_tensor_tensor(
+                out=sigma[:], in0=sigma[:], scalar=2.0, in1=relu[:], op0=ALU.mult, op1=ALU.add
+            )
+            nc.vector.tensor_mul(out=s2[:], in0=sigma[:], in1=sigma[:])
+            nc.vector.tensor_scalar_mul(out=s2[:], in0=s2[:], scalar1=-2.0)
+            nc.vector.reciprocal(out=neg_inv[:], in_=s2[:])
+            nc.vector.tensor_mul(out=exp_bias[:], in0=neg_inv[:], in1=m2[:])
+
+        m_grouped = const.tile([P, 4 * P], BF16, align_bytes=64)
+        m_codes = const.tile([P, P], U32, align_bytes=64)
+        m_scales = const.tile([P, P], U8, align_bytes=64)
+        m_state = {}
+
+        def means_to_k():
+            m_bank = psum.tile([P, 512], F32, tag="xm", bufs=1)
+            m_words = m_sb[:].bitcast(F32)
+            for u in range(2):
+                nc.tensor.transpose(m_bank[:, u * P : (u + 1) * P], m_words[:, u * P : (u + 1) * P], ident[:])
+            m_state["bank"] = m_bank
+
+        def means_copy_out():
+            nc.vector.tensor_copy(
+                out=m_grouped[:].bitcast(F32).rearrange("p (b u) -> p b u", u=2),
+                in_=m_state["bank"][:, 0 : 2 * P].rearrange("p (u b) -> p b u", u=2),
+            )
+
+        def means_quantise():
+            nc.vector.quantize_mx(out=m_codes[:].bitcast(FP8X4), scales=m_scales[:], in_=m_grouped[:])
+
+        res = const.tile([P, N_QUADS * QUAD * O], F32)
+        out_v = out.rearrange("(c p j) o -> p c (j o)", p=P, j=ROWS_PER_PART)
+        res_v = res[:].rearrange("p (c f) -> p c f", f=ROWS_PER_PART * O)
+
+        t1 = {}
+        x2 = {}
+        grouped = {}
+        codes = {}
+        scales = {}
+        xm = {}
+        dn = {}
+        dnt = {}
+        gall = {}
+        back = {}
+        sums = {}
+        best = {}
+
+        def live(q):
+            return 0 <= q < N_QUADS
+
+        for q in range(N_QUADS):
+            x2[q] = const.tile([P, QUAD], F32, name="x2_%d" % q)
+
+        def square_scalar(q, jj):
+            junk = work.tile([P, D], BF16, name="junk", bufs=2)
+            nc.scalar.activation(
+                out=junk[:], in_=xq[q][:, jj * D : (jj + 1) * D], func=ACT.Square, accum_out=x2[q][:, jj : jj + 1]
+            )
+
+        g_sq = const.tile([P, QUAD * D], F32)
+        g_sum = [const.tile([P, QUAD * (D >> (i + 1))], F32, name="g_sum%d" % i) for i in range(4)]
+        g_gate = const.tile([P, 1], F32)
+
+        def g_square(q, jj):
+            blk = xq[q][:, jj * D : (jj + 1) * D]
+            nc.gpsimd.tensor_tensor(out=g_sq[:, jj * D : (jj + 1) * D], in0=blk, in1=blk, op=ALU.mult)
+
+        def g_halve(level, first, count):
+            src = g_sq if level == 0 else g_sum[level - 1]
+            half = D >> (level + 1)
+            rows = src[:].rearrange("p (j n) -> p j n", n=2 * half)[:, first : first + count, :]
+            nc.gpsimd.tensor_tensor(
+                out=g_sum[level][:].rearrange("p (j n) -> p j n", n=half)[:, first : first + count, :],
+                in0=rows[:, :, 0:half], in1=rows[:, :, half : 2 * half], op=ALU.add,
+            )
+
+        def g_piece(q, i):
+            if i < QUAD:
+                g_square(q, i)
+            elif i < QUAD + 2:
+                g_halve(0, 2 * (i - QUAD), 2)
+            elif i == QUAD + 2:
+                g_halve(1, 0, QUAD)
+            else:
+                g_halve(2, 0, QUAD)
+                g_halve(3, 0, QUAD)
+
+        def g_finish(q):
+            nc.vector.tensor_reduce(
+                out=x2[q][:], in_=g_sum[3][:].rearrange("p (j n) -> p j n", n=D >> 4), op=ALU.add, axis=AX.X
+            )
+
+        def to_k(q):
+            if not live(q):
+                return
+            xw = xq[q][:].bitcast(F32)
+            t1[q] = []
+            for half in range(2):
+                bank = psum.tile([P, 512], F32, tag="t1", bufs=2)
+                for k in range(2):
+                    for u in range(2):
+                        first = (half * 2 + k) * WORDS + u * P
+                        slot = k * 2 + u
+                        nc.tensor.transpose(bank[:, slot * P : (slot + 1) * P], xw[:, first : first + P], ident[:])
+                t1[q].append(bank)
+
+        def copy_out(q, half):
+            if not live(q):
+                return
+            if half == 0:
+                g = work.tile([P, QUAD * 4 * P], BF16, name="g", align_bytes=64)
+                grouped[q] = g
+            gw = grouped[q][:].bitcast(F32)
+            dst = gw[:, half * 512 : (half + 1) * 512].rearrange("p (k b u) -> p k b u", k=2, u=2)
+            src = t1[q][half][:].rearrange("p (k u b) -> p k b u", k=2, u=2)
+            if half == 1 and q in S_COPIES:
+                nc.scalar.copy(out=dst, in_=src)
+            else:
+                nc.vector.tensor_copy(out=dst, in_=src)
+
+        def quantise(q):
+            if not live(q):
+                return
+            cd = work.tile([P, QUAD * P], U32, name="cd", align_bytes=64)
+            sc = work.tile([P, QUAD * P], U8, name="sc", align_bytes=64)
+            nc.vector.quantize_mx(out=cd[:].bitcast(FP8X4), scales=sc[:], in_=grouped[q][:])
+            codes[q] = cd
+            scales[q] = sc
+
+        def multiply(q):
+            if not live(q):
+                return
+            bank = psum.tile([P, 512], F32, tag="xm", bufs=1)
+            nc.tensor.matmul_mx(
+                out=bank[:],
+                lhsT=codes[q][:, 0:P].bitcast(FP8X4), lhsT_scale=scales[q][:, 0:P],
+                rhs=codes[q][:].bitcast(FP8X4), rhs_scale=scales[q][:],
+                start=True, stop=True,
+            )
+            for jj in range(QUAD):
+                cols = slice(jj * P, (jj + 1) * P)
+                nc.tensor.matmul_mx(
+                    out=bank[:, cols],
+                    lhsT=codes[q][:, cols].bitcast(FP8X4), lhsT_scale=scales[q][:, cols],
+                    rhs=m_codes[:].bitcast(FP8X4), rhs_scale=m_scales[:],
+                    start=True, stop=True,
+                )
+            xm[q] = bank
+
+        def add_x2(q):
+            if not live(q):
+                return
+            d = work.tile([P, QUAD * P], F32, name="d")
+            nc.vector.scalar_tensor_tensor(
+                out=d[:].rearrange("p (j n) -> p j n", n=P),
+                in0=xm[q][:].rearrange("p (j n) -> p j n", n=P),
+                scalar=-2.0,
+                in1=x2[q][:].unsqueeze(2).to_broadcast([P, QUAD, P]),
+                op0=ALU.mult, op1=ALU.add,
+            )
+            dn[q] = d
+
+        def to_centres(q):
+            if not live(q):
+                return
+            bank = psum.tile([P, 512], F32, tag="dnt", bufs=2)
+            for jj in range(QUAD):
+                nc.tensor.transpose(bank[:, jj * P : (jj + 1) * P], dn[q][:, jj * P : (jj + 1) * P], ident[:])
+            dnt[q] = bank
+
+        def gaussians(q):
+            if not live(q):
+                return
+            e = work.tile([P, QUAD * P], F32, name="e")
+            nc.scalar.activation(out=e[:], in_=dnt[q][:], func=ACT.Exp, scale=neg_inv[:], bias=exp_bias[:])
+            gall[q] = e
+
+        def to_rows(q):
+            if not live(q):
+                return
+            bank = psum.tile([P, 512], F32, tag="back", bufs=1)
+            for jj in range(QUAD):
+                nc.tensor.transpose(bank[:, jj * P : (jj + 1) * P], gall[q][:, jj * P : (jj + 1) * P], ident[:])
+            back[q] = bank
+            grp, i = divmod(q, GROUP)
+            if i == 0:
+                sbank = psum.tile([P, 512], F32, tag="sums", bufs=2)
+                sums[grp] = sbank
+            for jj in range(QUAD):
+                first = (i * QUAD + jj) * O
+                nc.tensor.matmul(
+                    out=sums[grp][:, first : first + SUM_COLS],
+                    lhsT=gall[q][:, jj * P : (jj + 1) * P], rhs=class_sum[:], start=True, stop=True,
+                )
+
+        def finish(q):
+            if not live(q):
+                return
+            grp, i = divmod(q, GROUP)
+            if i == 0:
+                bt = work.tile([P, GROUP * QUAD * O], F32, name="bt", bufs=2)
+                best[grp] = bt
+            nc.vector.tensor_reduce(
+                out=best[grp][:, i * QUAD * O : (i + 1) * QUAD * O],
+                in_=back[q][:].rearrange("p (g c) -> p g c", c=C)[:, :, 0:NC],
+                op=ALU.max, axis=AX.X,
+            )
+            if i == GROUP - 1:
+                width = GROUP * QUAD * O
+                nc.vector.scalar_tensor_tensor(
+                    out=res[:, grp * width : (grp + 1) * width].rearrange("p (b o) -> p b o", o=O),
+                    in0=best[grp][:].rearrange("p (b o) -> p b o", o=O),
+                    scalar=(NC + 1.0) / NC,
+                    in1=sums[grp][:, 0:width].rearrange("p (b o) -> p b o", o=O),
+                    op0=ALU.mult, op1=ALU.subtract,
+                )
+                nc.sync.dma_start(out=out_v[:, 2 * grp : 2 * grp + 2, :], in_=res_v[:, 2 * grp : 2 * grp + 2, :])
+
+        s_squares = [(q, jj) for q in range(N_QUADS) if q not in G_QUADS for jj in range(QUAD)]
+        g_pieces = [(q, i) for q in G_QUADS for i in range(8)]
+        s_done = 0
+        for s in range(-1, N_QUADS + 3):
+            to_rows(s - 3)
+            copy_out(s, 0)
+            if s == 0:
+                means_copy_out()
+            copy_out(s, 1)
+            to_k(s + 1)
+            if s == -1:
+                means_to_k()
+            if s == 0:
+                means_quantise()
+            if s == 2:
+                widths()
+            add_x2(s - 1)
+            to_centres(s - 1)
+            quantise(s)
+            multiply(s)
+            finish(s - 3)
+            g_index = s - G_FIRST_STEP
+            if 0 <= g_index < len(g_pieces):
+                nc.gpsimd.tensor_copy(out=g_gate[:], in_=codes[s][:, 0:1].bitcast(F32))
+                g_piece(g_pieces[g_index][0], g_pieces[g_index][1])
+            if 0 <= g_index - 1 < len(g_pieces) and g_pieces[g_index - 1][1] == 7:
+                g_finish(g_pieces[g_index - 1][0])
+            due = len([1 for (q, jj) in s_squares if q <= s])
+            even = int(round(S_LEAD + (s - 2) * len(s_squares) / N_QUADS))
+            while s_done < min(len(s_squares), max(due, even)):
+                square_scalar(s_squares[s_done][0], s_squares[s_done][1])
+                s_done += 1
+            if s == 0:
+                nc.scalar.activation(out=m_junk[:], in_=m_sb[:], func=ACT.Square, accum_out=m2[:])
+            gaussians(s - 2)

@@ -24,7 +24,8 @@ QUAD = 4
 N_QUADS = B // (QUAD * P)
 GROUP = 4
 WORDS = D // 2
-SUM_COLS = 48
+POS = O * NC
+BACK_COLS = POS + O
 SERIES = 11
 G_QUADS = (9, 17, 25)
 G_FIRST_STEP = 1
@@ -45,7 +46,11 @@ def tile_vertical_space_layer_t_kernel(tc, x, means, rho, out):
 
         rho_sb = const.tile([P, 1], BF16)
         with nc.allow_non_contiguous_dma(reason="128 single bf16 values, once"):
-            nc.scalar.dma_start(out=rho_sb[:], in_=rho.rearrange("o (c u) -> (o c) u", u=1))
+            for h in range(2):
+                nc.scalar.dma_start(
+                    out=rho_sb[h * POS : (h + 1) * POS, :],
+                    in_=rho[:, h * NC : (h + 1) * NC].rearrange("o (c u) -> o c u", u=1),
+                )
         m_sb = const.tile([P, D], BF16)
         xq = {}
         load_order = [0, 1, 2, G_QUADS[0]] + [q for q in range(3, N_QUADS) if q != G_QUADS[0]]
@@ -57,7 +62,8 @@ def tile_vertical_space_layer_t_kernel(tc, x, means, rho, out):
             if q == 0:
                 for jj in range(QUAD):
                     nc.sync.dma_start(out=dst[:, jj : jj + 1, :], in_=src[:, jj : jj + 1, :])
-                nc.sync.dma_start(out=m_sb[:], in_=means.rearrange("o c d -> (o c) d"))
+                for h in range(2):
+                    nc.sync.dma_start(out=m_sb[h * POS : (h + 1) * POS, :], in_=means[:, h * NC : (h + 1) * NC, :])
             else:
                 nc.sync.dma_start(out=dst, in_=src[:, h * QUAD : (h + 1) * QUAD, :])
             xq[q] = xt
@@ -70,11 +76,11 @@ def tile_vertical_space_layer_t_kernel(tc, x, means, rho, out):
         make_identity(nc, ident[:])
         class8 = const.tile([P, O], F32)
         nc.vector.tensor_reduce(
-            out=class8[:], in_=ident[:].rearrange("p (o c) -> p o c", c=C), op=ALU.add, axis=AX.X
+            out=class8[:], in_=ident[:].rearrange("p (h o c) -> p o h c", h=2, c=NC), op=ALU.add, axis=AX.XY
         )
-        class_sum = const.tile([P, SUM_COLS], F32)
-        nc.vector.memset(class_sum[:], 0.0)
-        nc.vector.tensor_scalar_mul(out=class_sum[:, 0:O], in0=class8[:], scalar1=1.0 / NC)
+        back_sum = const.tile([P, BACK_COLS], F32)
+        nc.vector.tensor_copy(out=back_sum[:, 0:POS], in_=ident[:, 0:POS])
+        nc.vector.tensor_scalar_mul(out=back_sum[:, POS:BACK_COLS], in0=class8[:], scalar1=1.0 / NC)
 
         rho_f = const.tile([P, 1], F32)
         nc.vector.tensor_copy(out=rho_f[:], in_=rho_sb[:])
@@ -122,23 +128,24 @@ def tile_vertical_space_layer_t_kernel(tc, x, means, rho, out):
             nc.vector.reciprocal(out=neg_inv[:], in_=s2[:])
             nc.vector.tensor_mul(out=exp_bias[:], in0=neg_inv[:], in1=m2[:])
 
-        m_grouped = const.tile([P, 4 * P], BF16, align_bytes=64)
-        m_codes = const.tile([P, P], U32, align_bytes=64)
-        m_scales = const.tile([P, P], U8, align_bytes=64)
+        m_grouped = const.tile([P, 2 * 4 * P], BF16, align_bytes=64)
+        m_codes = const.tile([P, 2 * P], U32, align_bytes=64)
+        m_scales = const.tile([P, 2 * P], U8, align_bytes=64)
         m_state = {}
 
         def means_to_k():
-            m_bank = psum.tile([P, 512], F32, tag="xm", bufs=1)
+            m_bank = psum.tile([P, 512], F32, tag="xm", bufs=2)
             m_words = m_sb[:].bitcast(F32)
             for u in range(2):
                 nc.tensor.transpose(m_bank[:, u * P : (u + 1) * P], m_words[:, u * P : (u + 1) * P], ident[:])
             m_state["bank"] = m_bank
 
         def means_copy_out():
-            nc.vector.tensor_copy(
-                out=m_grouped[:].bitcast(F32).rearrange("p (b u) -> p b u", u=2),
-                in_=m_state["bank"][:, 0 : 2 * P].rearrange("p (u b) -> p b u", u=2),
-            )
+            for r in range(2):
+                nc.vector.tensor_copy(
+                    out=m_grouped[:].bitcast(F32)[:, r * 2 * P : (r + 1) * 2 * P].rearrange("p (b u) -> p b u", u=2),
+                    in_=m_state["bank"][:, 0 : 2 * P].rearrange("p (u b) -> p b u", u=2),
+                )
 
         def means_quantise():
             nc.vector.quantize_mx(out=m_codes[:].bitcast(FP8X4), scales=m_scales[:], in_=m_grouped[:])
@@ -157,7 +164,6 @@ def tile_vertical_space_layer_t_kernel(tc, x, means, rho, out):
         dnt = {}
         gall = {}
         back = {}
-        sums = {}
         best = {}
 
         def live(q):
@@ -245,19 +251,14 @@ def tile_vertical_space_layer_t_kernel(tc, x, means, rho, out):
         def multiply(q):
             if not live(q):
                 return
-            bank = psum.tile([P, 512], F32, tag="xm", bufs=1)
-            nc.tensor.matmul_mx(
-                out=bank[:],
-                lhsT=codes[q][:, 0:P].bitcast(FP8X4), lhsT_scale=scales[q][:, 0:P],
-                rhs=codes[q][:].bitcast(FP8X4), rhs_scale=scales[q][:],
-                start=True, stop=True,
-            )
+            bank = psum.tile([P, 512], F32, tag="xm", bufs=2)
             for jj in range(QUAD):
                 cols = slice(jj * P, (jj + 1) * P)
+                width = min(2 * P, (QUAD - jj) * P)
                 nc.tensor.matmul_mx(
-                    out=bank[:, cols],
+                    out=bank[:, jj * P : jj * P + width],
                     lhsT=codes[q][:, cols].bitcast(FP8X4), lhsT_scale=scales[q][:, cols],
-                    rhs=m_codes[:].bitcast(FP8X4), rhs_scale=m_scales[:],
+                    rhs=m_codes[:, 0:width].bitcast(FP8X4), rhs_scale=m_scales[:, 0:width],
                     start=True, stop=True,
                 )
             xm[q] = bank
@@ -293,52 +294,56 @@ def tile_vertical_space_layer_t_kernel(tc, x, means, rho, out):
         def to_rows(q):
             if not live(q):
                 return
-            bank = psum.tile([P, 512], F32, tag="back", bufs=1)
+            bank = psum.tile([P, 512], F32, tag="back", bufs=2)
             for jj in range(QUAD):
-                nc.tensor.transpose(bank[:, jj * P : (jj + 1) * P], gall[q][:, jj * P : (jj + 1) * P], ident[:])
-            back[q] = bank
-            grp, i = divmod(q, GROUP)
-            if i == 0:
-                sbank = psum.tile([P, 512], F32, tag="sums", bufs=2)
-                sums[grp] = sbank
+                block = gall[q][:, jj * P : (jj + 1) * P]
+                first = jj * P
+                if (q * QUAD + jj) % 3 == 2:
+                    nc.tensor.transpose(bank[:, first : first + P], block, ident[:])
             for jj in range(QUAD):
-                first = (i * QUAD + jj) * O
+                block = gall[q][:, jj * P : (jj + 1) * P]
+                first = jj * P
+                skip = POS if (q * QUAD + jj) % 3 == 2 else 0
                 nc.tensor.matmul(
-                    out=sums[grp][:, first : first + SUM_COLS],
-                    lhsT=gall[q][:, jj * P : (jj + 1) * P], rhs=class_sum[:], start=True, stop=True,
+                    out=bank[:, first + skip : first + BACK_COLS],
+                    lhsT=block, rhs=back_sum[:, skip:BACK_COLS], start=True, stop=True,
                 )
+            back[q] = bank
 
         def finish(q):
             if not live(q):
                 return
-            grp, i = divmod(q, GROUP)
-            if i == 0:
-                bt = work.tile([P, GROUP * QUAD * O], F32, name="bt", bufs=2)
-                best[grp] = bt
+            bt = work.tile([P, QUAD * O], F32, name="bt")
             nc.vector.tensor_reduce(
-                out=best[grp][:, i * QUAD * O : (i + 1) * QUAD * O],
-                in_=back[q][:].rearrange("p (g c) -> p g c", c=C)[:, :, 0:NC],
+                out=bt[:].rearrange("p (j o) -> p j o", o=O),
+                in_=back[q][:].rearrange("p (j n) -> p j n", n=P)[:, :, 0:POS].rearrange("p j (o c) -> p j o c", c=NC),
                 op=ALU.max, axis=AX.X,
             )
+            best[q] = bt
+
+        def combine(q):
+            if not live(q):
+                return
+            grp, i = divmod(q, GROUP)
+            nc.vector.scalar_tensor_tensor(
+                out=res[:, q * QUAD * O : (q + 1) * QUAD * O].rearrange("p (j o) -> p j o", o=O),
+                in0=best[q][:].rearrange("p (j o) -> p j o", o=O),
+                scalar=(NC + 1.0) / NC,
+                in1=back[q][:].rearrange("p (j n) -> p j n", n=P)[:, :, POS:BACK_COLS],
+                op0=ALU.mult, op1=ALU.subtract,
+            )
             if i == GROUP - 1:
-                width = GROUP * QUAD * O
-                nc.vector.scalar_tensor_tensor(
-                    out=res[:, grp * width : (grp + 1) * width].rearrange("p (b o) -> p b o", o=O),
-                    in0=best[grp][:].rearrange("p (b o) -> p b o", o=O),
-                    scalar=(NC + 1.0) / NC,
-                    in1=sums[grp][:, 0:width].rearrange("p (b o) -> p b o", o=O),
-                    op0=ALU.mult, op1=ALU.subtract,
-                )
                 nc.sync.dma_start(out=out_v[:, 2 * grp : 2 * grp + 2, :], in_=res_v[:, 2 * grp : 2 * grp + 2, :])
 
         s_squares = [(q, jj) for q in range(N_QUADS) if q not in G_QUADS for jj in range(QUAD)]
         g_pieces = [(q, i) for q in G_QUADS for i in range(8)]
         s_done = 0
-        for s in range(-1, N_QUADS + 3):
+        for s in range(-1, N_QUADS + 4):
             to_rows(s - 3)
             copy_out(s, 0)
             if s == 0:
                 means_copy_out()
+            combine(s - 4)
             copy_out(s, 1)
             to_k(s + 1)
             if s == -1:

from contextlib import ExitStack

import concourse.mybir as mybir
from concourse.masks import make_identity

F32 = mybir.dt.float32
BF16 = mybir.dt.bfloat16
U32 = mybir.dt.uint32
U8 = mybir.dt.uint8
FP8X4 = mybir.dt.float8_e4m3fn_x4
ACT = mybir.ActivationFunctionType
ALU = mybir.AluOpType
AX = mybir.AxisListType

P = 128
B = 16384
D = 512
O = 8
C = 16
NC = 8
ROWS_PER_PART = 8
CHUNK = P * ROWS_PER_PART
QUAD = 4
N_QUADS = B // (QUAD * P)
GROUP = 4
WORDS = D // 2
POS = O * NC
BACK_COLS = POS + O
SERIES = 11
G_QUADS = (9, 17, 25)
G_FIRST_STEP = 1
S_COPIES = (6, 11, 16, 21, 26)
S_LEAD = 14

FLOPS = 2 * B * O * C * D


def tile_vertical_space_layer_t_kernel(tc, x, means, rho, out):
    nc = tc.nc
    with ExitStack() as ctx:
        const = ctx.enter_context(tc.tile_pool(name="const", bufs=1))
        xpool = ctx.enter_context(tc.tile_pool(name="xpool", bufs=N_QUADS))
        work = ctx.enter_context(tc.tile_pool(name="work", bufs=3))
        psum = ctx.enter_context(tc.psum_pool(name="psum", bufs=1))
        ctx.enter_context(tc.manual_schedule())

        rho_sb = const.tile([P, 1], BF16)
        with nc.allow_non_contiguous_dma(reason="128 single bf16 values, once"):
            for h in range(2):
                nc.scalar.dma_start(
                    out=rho_sb[h * POS : (h + 1) * POS, :],
                    in_=rho[:, h * NC : (h + 1) * NC].rearrange("o (c u) -> o c u", u=1),
                )
        m_sb = const.tile([P, D], BF16)
        xq = {}
        load_order = [0, 1, 2, G_QUADS[0]] + [q for q in range(3, N_QUADS) if q != G_QUADS[0]]
        for q in load_order:
            c, h = divmod(q, ROWS_PER_PART // QUAD)
            xt = xpool.tile([P, QUAD * D], BF16, name="xt")
            src = x[c * CHUNK : (c + 1) * CHUNK, :].rearrange("(p j) d -> p j d", j=ROWS_PER_PART)
            dst = xt[:].rearrange("p (j d) -> p j d", d=D)
            if q == 0:
                for jj in range(QUAD):
                    nc.sync.dma_start(out=dst[:, jj : jj + 1, :], in_=src[:, jj : jj + 1, :])
                for h in range(2):
                    nc.sync.dma_start(out=m_sb[h * POS : (h + 1) * POS, :], in_=means[:, h * NC : (h + 1) * NC, :])
            else:
                nc.sync.dma_start(out=dst, in_=src[:, h * QUAD : (h + 1) * QUAD, :])
            xq[q] = xt

        one = const.tile([P, 1], F32)
        nc.vector.memset(one[:], 1.0)
        warm = const.tile([P, 1], F32)
        nc.scalar.activation(out=warm[:], in_=one[:], func=ACT.Exp)
        ident = const.tile([P, P], F32)
        make_identity(nc, ident[:])
        class8 = const.tile([P, O], F32)
        nc.vector.tensor_reduce(
            out=class8[:], in_=ident[:].rearrange("p (h o c) -> p o h c", h=2, c=NC), op=ALU.add, axis=AX.XY
        )
        back_sum = const.tile([P, BACK_COLS], F32)
        nc.vector.tensor_copy(out=back_sum[:, 0:POS], in_=ident[:, 0:POS])
        nc.vector.tensor_scalar_mul(out=back_sum[:, POS:BACK_COLS], in0=class8[:], scalar1=1.0 / NC)

        rho_f = const.tile([P, 1], F32)
        nc.vector.tensor_copy(out=rho_f[:], in_=rho_sb[:])
        rho_n = const.tile([P, 1], F32)
        nc.vector.tensor_scalar_mul(out=rho_n[:], in0=rho_f[:], scalar1=-1.0)
        nabs = const.tile([P, 1], F32)
        nc.vector.tensor_tensor(out=nabs[:], in0=rho_f[:], in1=rho_n[:], op=ALU.min)
        relu = const.tile([P, 1], F32)
        nc.vector.tensor_scalar_max(out=relu[:], in0=rho_f[:], scalar1=0.0)
        t_small = const.tile([P, 1], F32)
        nc.scalar.activation(out=t_small[:], in_=nabs[:], func=ACT.Exp)
        den = const.tile([P, 1], F32)
        nc.vector.tensor_scalar_add(out=den[:], in0=t_small[:], scalar1=2.0)
        rden = const.tile([P, 1], F32)
        nc.vector.reciprocal(out=rden[:], in_=den[:])
        u_small = const.tile([P, 1], F32)
        nc.vector.tensor_mul(out=u_small[:], in0=t_small[:], in1=rden[:])
        u2 = const.tile([P, 1], F32)
        nc.vector.tensor_mul(out=u2[:], in0=u_small[:], in1=u_small[:])
        horner = [const.tile([P, 1], F32, name="horner%d" % i) for i in range(2)]
        nc.gpsimd.tensor_scalar(
            out=horner[0][:], in0=u2[:], scalar1=1.0 / (2 * SERIES - 1), scalar2=1.0 / (2 * SERIES - 3),
            op0=ALU.mult, op1=ALU.add,
        )
        for i in range(SERIES - 2):
            nc.gpsimd.tensor_scalar(
                out=horner[(i + 1) % 2][:], in0=horner[i % 2][:], scalar1=u2[:], scalar2=1.0 / (2 * (SERIES - 3 - i) + 1),
                op0=ALU.mult, op1=ALU.add,
            )
        series = horner[(SERIES - 2) % 2]
        m2 = const.tile([P, 1], F32)
        m_junk = const.tile([P, D], BF16)
        sigma = const.tile([P, 1], F32)
        s2 = const.tile([P, 1], F32)
        neg_inv = const.tile([P, 1], F32)
        exp_bias = const.tile([P, 1], F32)

        def widths():
            nc.vector.tensor_mul(out=sigma[:], in0=u_small[:], in1=series[:])
            nc.vector.scalar_tensor_tensor(
                out=sigma[:], in0=sigma[:], scalar=2.0, in1=relu[:], op0=ALU.mult, op1=ALU.add
            )
            nc.vector.tensor_mul(out=s2[:], in0=sigma[:], in1=sigma[:])
            nc.vector.tensor_scalar_mul(out=s2[:], in0=s2[:], scalar1=-2.0)
            nc.vector.reciprocal(out=neg_inv[:], in_=s2[:])
            nc.vector.tensor_mul(out=exp_bias[:], in0=neg_inv[:], in1=m2[:])

        m_grouped = const.tile([P, 2 * 4 * P], BF16, align_bytes=64)
        m_codes = const.tile([P, 2 * P], U32, align_bytes=64)
        m_scales = const.tile([P, 2 * P], U8, align_bytes=64)
        m_state = {}

        def means_to_k():
            m_bank = psum.tile([P, 512], F32, tag="xm", bufs=2)
            m_words = m_sb[:].bitcast(F32)
            for u in range(2):
                nc.tensor.transpose(m_bank[:, u * P : (u + 1) * P], m_words[:, u * P : (u + 1) * P], ident[:])
            m_state["bank"] = m_bank

        def means_copy_out():
            for r in range(2):
                nc.vector.tensor_copy(
                    out=m_grouped[:].bitcast(F32)[:, r * 2 * P : (r + 1) * 2 * P].rearrange("p (b u) -> p b u", u=2),
                    in_=m_state["bank"][:, 0 : 2 * P].rearrange("p (u b) -> p b u", u=2),
                )

        def means_quantise():
            nc.vector.quantize_mx(out=m_codes[:].bitcast(FP8X4), scales=m_scales[:], in_=m_grouped[:])

        res = const.tile([P, N_QUADS * QUAD * O], F32)
        out_v = out.rearrange("(c p j) o -> p c (j o)", p=P, j=ROWS_PER_PART)
        res_v = res[:].rearrange("p (c f) -> p c f", f=ROWS_PER_PART * O)

        t1 = {}
        x2 = {}
        grouped = {}
        codes = {}
        scales = {}
        xm = {}
        dn = {}
        dnt = {}
        gall = {}
        back = {}
        best = {}

        def live(q):
            return 0 <= q < N_QUADS

        for q in range(N_QUADS):
            x2[q] = const.tile([P, QUAD], F32, name="x2_%d" % q)

        def square_scalar(q, jj):
            junk = work.tile([P, D], BF16, name="junk", bufs=2)
            nc.scalar.activation(
                out=junk[:], in_=xq[q][:, jj * D : (jj + 1) * D], func=ACT.Square, accum_out=x2[q][:, jj : jj + 1]
            )

        g_sq = const.tile([P, QUAD * D], F32)
        g_sum = [const.tile([P, QUAD * (D >> (i + 1))], F32, name="g_sum%d" % i) for i in range(4)]
        g_gate = const.tile([P, 1], F32)

        def g_square(q, jj):
            blk = xq[q][:, jj * D : (jj + 1) * D]
            nc.gpsimd.tensor_tensor(out=g_sq[:, jj * D : (jj + 1) * D], in0=blk, in1=blk, op=ALU.mult)

        def g_halve(level, first, count):
            src = g_sq if level == 0 else g_sum[level - 1]
            half = D >> (level + 1)
            rows = src[:].rearrange("p (j n) -> p j n", n=2 * half)[:, first : first + count, :]
            nc.gpsimd.tensor_tensor(
                out=g_sum[level][:].rearrange("p (j n) -> p j n", n=half)[:, first : first + count, :],
                in0=rows[:, :, 0:half], in1=rows[:, :, half : 2 * half], op=ALU.add,
            )

        def g_piece(q, i):
            if i < QUAD:
                g_square(q, i)
            elif i < QUAD + 2:
                g_halve(0, 2 * (i - QUAD), 2)
            elif i == QUAD + 2:
                g_halve(1, 0, QUAD)
            else:
                g_halve(2, 0, QUAD)
                g_halve(3, 0, QUAD)

        def g_finish(q):
            nc.vector.tensor_reduce(
                out=x2[q][:], in_=g_sum[3][:].rearrange("p (j n) -> p j n", n=D >> 4), op=ALU.add, axis=AX.X
            )

        def to_k(q):
            if not live(q):
                return
            xw = xq[q][:].bitcast(F32)
            t1[q] = []
            for half in range(2):
                bank = psum.tile([P, 512], F32, tag="t1", bufs=2)
                for k in range(2):
                    for u in range(2):
                        first = (half * 2 + k) * WORDS + u * P
                        slot = k * 2 + u
                        nc.tensor.transpose(bank[:, slot * P : (slot + 1) * P], xw[:, first : first + P], ident[:])
                t1[q].append(bank)

        def copy_out(q, half):
            if not live(q):
                return
            if half == 0:
                g = work.tile([P, QUAD * 4 * P], BF16, name="g", align_bytes=64)
                grouped[q] = g
            gw = grouped[q][:].bitcast(F32)
            dst = gw[:, half * 512 : (half + 1) * 512].rearrange("p (k b u) -> p k b u", k=2, u=2)
            src = t1[q][half][:].rearrange("p (k u b) -> p k b u", k=2, u=2)
            if half == 1 and q in S_COPIES:
                nc.scalar.copy(out=dst, in_=src)
            else:
                nc.vector.tensor_copy(out=dst, in_=src)

        def quantise(q):
            if not live(q):
                return
            cd = work.tile([P, QUAD * P], U32, name="cd", align_bytes=64)
            sc = work.tile([P, QUAD * P], U8, name="sc", align_bytes=64)
            nc.vector.quantize_mx(out=cd[:].bitcast(FP8X4), scales=sc[:], in_=grouped[q][:])
            codes[q] = cd
            scales[q] = sc

        def multiply(q):
            if not live(q):
                return
            bank = psum.tile([P, 512], F32, tag="xm", bufs=2)
            for jj in range(QUAD):
                cols = slice(jj * P, (jj + 1) * P)
                width = min(2 * P, (QUAD - jj) * P)
                nc.tensor.matmul_mx(
                    out=bank[:, jj * P : jj * P + width],
                    lhsT=codes[q][:, cols].bitcast(FP8X4), lhsT_scale=scales[q][:, cols],
                    rhs=m_codes[:, 0:width].bitcast(FP8X4), rhs_scale=m_scales[:, 0:width],
                    start=True, stop=True,
                )
            xm[q] = bank

        def add_x2(q):
            if not live(q):
                return
            d = work.tile([P, QUAD * P], F32, name="d")
            nc.vector.scalar_tensor_tensor(
                out=d[:].rearrange("p (j n) -> p j n", n=P),
                in0=xm[q][:].rearrange("p (j n) -> p j n", n=P),
                scalar=-2.0,
                in1=x2[q][:].unsqueeze(2).to_broadcast([P, QUAD, P]),
                op0=ALU.mult, op1=ALU.add,
            )
            dn[q] = d

        def to_centres(q):
            if not live(q):
                return
            bank = psum.tile([P, 512], F32, tag="dnt", bufs=2)
            for jj in range(QUAD):
                nc.tensor.transpose(bank[:, jj * P : (jj + 1) * P], dn[q][:, jj * P : (jj + 1) * P], ident[:])
            dnt[q] = bank

        def gaussians(q):
            if not live(q):
                return
            e = work.tile([P, QUAD * P], F32, name="e")
            nc.scalar.activation(out=e[:], in_=dnt[q][:], func=ACT.Exp, scale=neg_inv[:], bias=exp_bias[:])
            gall[q] = e

        def to_rows(q):
            if not live(q):
                return
            bank = psum.tile([P, 512], F32, tag="back", bufs=2)
            for jj in range(QUAD):
                block = gall[q][:, jj * P : (jj + 1) * P]
                first = jj * P
                if (q * QUAD + jj) % 3 == 2:
                    nc.tensor.transpose(bank[:, first : first + P], block, ident[:])
            for jj in range(QUAD):
                block = gall[q][:, jj * P : (jj + 1) * P]
                first = jj * P
                skip = POS if (q * QUAD + jj) % 3 == 2 else 0
                nc.tensor.matmul(
                    out=bank[:, first + skip : first + BACK_COLS],
                    lhsT=block, rhs=back_sum[:, skip:BACK_COLS], start=True, stop=True,
                )
            back[q] = bank

        def finish(q):
            if not live(q):
                return
            bt = work.tile([P, QUAD * O], F32, name="bt")
            nc.vector.tensor_reduce(
                out=bt[:].rearrange("p (j o) -> p j o", o=O),
                in_=back[q][:].rearrange("p (j n) -> p j n", n=P)[:, :, 0:POS].rearrange("p j (o c) -> p j o c", c=NC),
                op=ALU.max, axis=AX.X,
            )
            best[q] = bt

        def combine(q):
            if not live(q):
                return
            grp, i = divmod(q, GROUP)
            nc.vector.scalar_tensor_tensor(
                out=res[:, q * QUAD * O : (q + 1) * QUAD * O].rearrange("p (j o) -> p j o", o=O),
                in0=best[q][:].rearrange("p (j o) -> p j o", o=O),
                scalar=(NC + 1.0) / NC,
                in1=back[q][:].rearrange("p (j n) -> p j n", n=P)[:, :, POS:BACK_COLS],
                op0=ALU.mult, op1=ALU.subtract,
            )
            if i == GROUP - 1:
                nc.sync.dma_start(out=out_v[:, 2 * grp : 2 * grp + 2, :], in_=res_v[:, 2 * grp : 2 * grp + 2, :])

        s_squares = [(q, jj) for q in range(N_QUADS) if q not in G_QUADS for jj in range(QUAD)]
        g_pieces = [(q, i) for q in G_QUADS for i in range(8)]
        s_done = 0
        for s in range(-1, N_QUADS + 4):
            to_rows(s - 3)
            copy_out(s, 0)
            if s == 0:
                means_copy_out()
            combine(s - 4)
            copy_out(s, 1)
            to_k(s + 1)
            if s == -1:
                means_to_k()
            if s == 0:
                means_quantise()
            if s == 2:
                widths()
            add_x2(s - 1)
            to_centres(s - 1)
            quantise(s)
            multiply(s)
            finish(s - 3)
            g_index = s - G_FIRST_STEP
            if 0 <= g_index < len(g_pieces):
                nc.gpsimd.tensor_copy(out=g_gate[:], in_=codes[s][:, 0:1].bitcast(F32))
                g_piece(g_pieces[g_index][0], g_pieces[g_index][1])
            if 0 <= g_index - 1 < len(g_pieces) and g_pieces[g_index - 1][1] == 7:
                g_finish(g_pieces[g_index - 1][0])
            due = len([1 for (q, jj) in s_squares if q <= s])
            even = int(round(S_LEAD + (s - 2) * len(s_squares) / N_QUADS))
            while s_done < min(len(s_squares), max(due, even)):
                square_scalar(s_squares[s_done][0], s_squares[s_done][1])
                s_done += 1
            if s == 0:
                nc.scalar.activation(out=m_junk[:], in_=m_sb[:], func=ACT.Square, accum_out=m2[:])
            gaussians(s - 2)
